import numpy as np
import ml_dtypes


def mxq(x, axis, fmt="e4m3"):
    dtype, down = {"e4m3": (ml_dtypes.float8_e4m3fn, 7), "e5m2": (ml_dtypes.float8_e5m2, 14)}[fmt]
    v = np.moveaxis(np.asarray(x, np.float32).astype(ml_dtypes.bfloat16).astype(np.float64), axis, -1)
    blocks = v.reshape(v.shape[:-1] + (-1, 32))
    amax = np.abs(blocks).max(-1, keepdims=True)
    byte = np.maximum(np.where(amax > 0, np.frexp(amax)[1] - 1 + 127, 0) - down, 1)
    scale = np.exp2(byte - 127.0)
    codes = (blocks / scale).astype(np.float32).astype(dtype).astype(np.float64)
    return np.moveaxis((codes * scale).reshape(v.shape), -1, axis)


WIDE = False


def mx_kscale(k):
    if not WIDE:
        return np.ones(k)
    levels = np.array([10, -10, 5, -5, 0])
    a = np.random.permutation(np.resize(levels, k // 512 * 4)).reshape(k // 512, 4)
    idx = np.arange(k)
    return np.exp2(a[idx // 512, idx % 128 // 32])


BF16 = ml_dtypes.bfloat16


def bf(x):
    return np.asarray(x, np.float32).astype(BF16)


def f64(x):
    return np.asarray(x).astype(np.float64)


B, I, H = 256, 1024, 2048
DT = 0.1
STEPS = 2


def sigmoid(v):
    return 1.0 / (1.0 + np.exp(-v))


def setup_inputs():
    s = mx_kscale(H)
    r = np.minimum(s, 1.0)
    return {"h": bf(np.random.standard_normal((B, H)) * 0.7 * s),
            "input_contrib": bf(np.random.standard_normal((B, H)) * 0.9),
            "x_tau": bf(np.random.standard_normal((B, H)) * 0.9),
            "W_rec": bf(np.random.standard_normal((H, H)) * 1.0 / np.sqrt(H) / s),
            "tau_w_h": bf(np.random.standard_normal((H, H)) * 1.2 / np.sqrt(H) / s),
            "tau_adapt_b": bf(np.random.standard_normal(H) * 0.5),
            "tau_base": bf((0.3 + 0.3 * np.random.random(H)) / r)}


def reference(h, input_contrib, x_tau, W_rec, tau_w_h, tau_adapt_b, tau_base):
    h = f64(h)
    wr = mxq(f64(W_rec), 1, "e4m3")
    wt = mxq(f64(tau_w_h), 1, "e4m3")
    tau = None
    for _ in range(STEPS):
        hq = mxq(h, 1, "e4m3")
        tau_logits = f64(x_tau) + (hq @ wt.T) + f64(tau_adapt_b)
        tau = f64(tau_base) * (0.5 + sigmoid(tau_logits))
        activated = np.tanh((hq @ wr.T) + f64(input_contrib))
        h = h + DT * (-h + activated) / tau
    return (h, tau)

@@ -1,0 +1,329 @@
+from contextlib import ExitStack
+import math
+
+import concourse.masks as masks
+import concourse.mybir as mybir
+
+F32 = mybir.dt.float32
+BF16 = mybir.dt.bfloat16
+U32 = mybir.dt.uint32
+U8 = mybir.dt.uint8
+FP8X4 = mybir.dt.float8_e4m3fn_x4
+ALU = mybir.AluOpType
+ACT = mybir.ActivationFunctionType
+
+P = 128
+BATCH = 256
+HID = 2048
+DT = 0.1
+STEPS = 2
+BATCH_TILES = BATCH // P
+PAIR = 2
+K_PASS = 4 * P
+PASSES = HID // K_PASS
+CHUNK = PAIR * P
+CHUNKS = HID // CHUNK
+BANK = 512
+UNITS = 2 * CHUNKS
+STAGE_BUFS = 5
+DRAIN = 6
+
+FLOPS = 2 * STEPS * 2 * BATCH * HID * HID
+
+
+def tile_liquidcell_pb_kernel(
+    tc, h, input_contrib, x_tau, W_rec, tau_w_h, tau_adapt_b, tau_base, out_0, out_1
+):
+    nc = tc.nc
+    with ExitStack() as ctx:
+        keep = ctx.enter_context(tc.tile_pool(name="keep", bufs=1))
+        stage = ctx.enter_context(tc.tile_pool(name="stage", bufs=STAGE_BUFS))
+        group = ctx.enter_context(tc.tile_pool(name="group", bufs=2))
+        work = ctx.enter_context(tc.tile_pool(name="work", bufs=2))
+        psum_t = ctx.enter_context(tc.psum_pool(name="psum_t", bufs=4))
+        psum_a = ctx.enter_context(tc.psum_pool(name="psum_a", bufs=4))
+        ctx.enter_context(tc.manual_schedule())
+
+        weights = (tau_w_h, W_rec)
+        w_codes = [
+            keep.tile([P, CHUNKS, PASSES, PAIR, P], U32, name="w_codes%d" % w, align_bytes=64)
+            for w in range(2)
+        ]
+        w_scales = [
+            keep.tile([P, CHUNKS, PASSES, PAIR, P], U8, name="w_scales%d" % w, align_bytes=64)
+            for w in range(2)
+        ]
+        s_codes = [
+            keep.tile([P, PASSES, BATCH], U32, name="s_codes%d" % s, align_bytes=64)
+            for s in range(STEPS)
+        ]
+        s_scales = [
+            keep.tile([P, PASSES, BATCH], U8, name="s_scales%d" % s, align_bytes=64)
+            for s in range(STEPS)
+        ]
+        state_bf = keep.tile([P, PASSES, BATCH, 2 * PAIR], BF16, name="state_bf", align_bytes=64)
+        h1T = keep.tile([P, CHUNKS, PAIR, BATCH], F32, name="h1T")
+        xT = keep.tile([P, CHUNKS, BATCH * PAIR], BF16, name="xT")
+        icT = keep.tile([P, CHUNKS, BATCH * PAIR], BF16, name="icT")
+        addend = (xT, icT)
+
+        ident = keep.tile([P, P], F32, name="ident")
+        masks.make_identity(nc, ident[:])
+
+        def transpose_bank(words, i):
+            bank = psum_t.tile([P, BANK], F32, name="bank", tag="bank")
+            for v in range(2):
+                for r in range(2):
+                    slot = 2 * v + r
+                    block = 2 * i + v
+                    nc.tensor.transpose(
+                        bank[:, slot * P : (slot + 1) * P],
+                        words[:, r, block * P : (block + 1) * P],
+                        ident[:],
+                    )
+            return bank
+
+        vec_rows = keep.tile([P, PAIR * P], BF16, name="vec_rows")
+        nc.vector.memset(vec_rows[:], 0.0)
+        nc.scalar.dma_start(
+            out=vec_rows[0:CHUNKS, :], in_=tau_adapt_b.rearrange("(g w) -> g w", g=CHUNKS)
+        )
+        nc.scalar.dma_start(
+            out=vec_rows[CHUNKS : 2 * CHUNKS, :], in_=tau_base.rearrange("(g w) -> g w", g=CHUNKS)
+        )
+
+        def load_rows(rows):
+            staged = stage.tile([P, 2, HID], BF16, name="staged", tag="staged")
+            nc.sync.dma_start(out=staged[:], in_=rows)
+            return staged
+
+        staged_units = {}
+
+        def load_unit(a):
+            rows = weights[a % 2][(a // 2) * CHUNK : (a // 2 + 1) * CHUNK, :]
+            staged_units[a] = load_rows(rows.rearrange("(p e) k -> p e k", e=PAIR))
+
+        h_st = stage.tile([P, 2, HID], BF16, name="staged", tag="staged")
+        h_rows = h.rearrange("(t p) k -> p t k", p=P)
+        for g in range(PASSES):
+            nc.sync.dma_start(
+                out=h_st[:, :, g * K_PASS : (g + 1) * K_PASS],
+                in_=h_rows[:, :, g * K_PASS : (g + 1) * K_PASS],
+            )
+        x_st = load_rows(x_tau.rearrange("(t p) k -> p t k", p=P))
+        ic_st = load_rows(input_contrib.rearrange("(t p) k -> p t k", p=P))
+        for a in range(STAGE_BUFS - 3):
+            load_unit(a)
+
+        vec_bank = psum_t.tile([P, BANK], F32, name="bank", tag="bank")
+        nc.tensor.transpose(vec_bank[:, 0:P], vec_rows[:].bitcast(F32), ident[:])
+        vecs = keep.tile([P, 4 * CHUNKS], F32, name="vecs")
+        nc.vector.tensor_copy(out=vecs[:], in_=vec_bank[:, 0 : 2 * CHUNKS].bitcast(BF16))
+        b_col = vecs[:, 0 : 2 * CHUNKS]
+        tb_col = vecs[:, 2 * CHUNKS : 4 * CHUNKS]
+        bias_th = keep.tile([P, 2 * CHUNKS], F32, name="bias_th")
+        bias_t2 = keep.tile([P, 2 * CHUNKS], F32, name="bias_t2")
+        half_tb = keep.tile([P, 2 * CHUNKS], F32, name="half_tb")
+        neg_c = keep.tile([P, 2 * CHUNKS], F32, name="neg_c")
+        nc.vector.tensor_scalar(
+            out=bias_th[:], in0=b_col, scalar1=0.5, scalar2=0.0, op0=ALU.mult, op1=ALU.add
+        )
+        nc.vector.tensor_scalar(
+            out=bias_t2[:], in0=b_col, scalar1=0.5, scalar2=0.5 * math.log(3.0),
+            op0=ALU.mult, op1=ALU.add,
+        )
+        nc.vector.tensor_scalar(
+            out=half_tb[:], in0=tb_col, scalar1=0.5, scalar2=0.0, op0=ALU.mult, op1=ALU.add
+        )
+        nc.vector.reciprocal(out=neg_c[:], in_=tb_col)
+        nc.vector.tensor_scalar(
+            out=neg_c[:], in0=neg_c[:], scalar1=-DT * 2.0 / 3.0, scalar2=0.0,
+            op0=ALU.mult, op1=ALU.add,
+        )
+
+        def quantise_state(step, g):
+            nc.vector.quantize_mx(
+                out=s_codes[step][:, g, :].bitcast(FP8X4),
+                scales=s_scales[step][:, g, :],
+                in_=state_bf[:, g].rearrange("p b t -> p (b t)"),
+            )
+
+        state_words = state_bf[:].bitcast(F32)
+        for g in range(PASSES):
+            bank = transpose_bank(h_st[:].bitcast(F32), g)
+            nc.vector.tensor_copy(
+                out=state_words[:, g], in_=bank[:].rearrange("q (u b) -> q b u", u=2)
+            )
+        for staged, dest in ((x_st, xT), (ic_st, icT)):
+            for i in range(CHUNKS // 2):
+                bank = transpose_bank(staged[:].bitcast(F32), i)
+                nc.scalar.copy(
+                    out=dest[:].bitcast(F32)[:, 2 * i : 2 * i + 2, :],
+                    in_=bank[:].rearrange("q (v b) -> q v b", v=2),
+                )
+        for g in range(PASSES):
+            quantise_state(0, g)
+        for a in range(STAGE_BUFS - 3, STAGE_BUFS):
+            load_unit(a)
+
+        grouped_units = {}
+        accs = {}
+        pre = {}
+        gates = {}
+        half_tanh = {}
+        new_state = {}
+
+        def transpose_unit(a):
+            words = staged_units[a][:].bitcast(F32)
+            grouped = group.tile([P, PASSES, PAIR, P, 2 * PAIR], BF16, name="grouped", align_bytes=64)
+            for g in range(PASSES):
+                bank = transpose_bank(words, g)
+                nc.scalar.copy(
+                    out=grouped[:].bitcast(F32)[:, g],
+                    in_=bank[:].rearrange("q (u e p) -> q e p u", u=2, e=PAIR),
+                )
+            grouped_units[a] = grouped
+
+        def quantise_unit(a):
+            grouped = grouped_units[a]
+            nc.vector.quantize_mx(
+                out=w_codes[a % 2][:, a // 2].rearrange("q g e p -> q (g e p)").bitcast(FP8X4),
+                scales=w_scales[a % 2][:, a // 2].rearrange("q g e p -> q (g e p)"),
+                in_=grouped[:].rearrange("q g e p t -> q (g e p t)"),
+            )
+
+        def multiply_unit(step, a):
+            acc = psum_a.tile([P, PAIR, BATCH], F32, name="acc", tag="acc")
+            for e in range(PAIR):
+                for g in range(PASSES):
+                    nc.tensor.matmul_mx(
+                        out=acc[:, e, :],
+                        lhsT=w_codes[a % 2][:, a // 2, g, e, :].bitcast(FP8X4),
+                        lhsT_scale=w_scales[a % 2][:, a // 2, g, e, :],
+                        rhs=s_codes[step][:, g, :].bitcast(FP8X4),
+                        rhs_scale=s_scales[step][:, g, :],
+                        start=(g == 0),
+                        stop=(g == PASSES - 1),
+                    )
+            accs[a] = acc
+
+        def add_unit(a):
+            summed = work.tile([P, PAIR, BATCH], F32, name="summed%d" % (a % 2))
+            nc.vector.tensor_tensor(
+                out=summed[:],
+                in0=accs[a][:],
+                in1=addend[a % 2][:, a // 2, :].rearrange("p (b e) -> p e b", e=PAIR),
+                op=ALU.add,
+            )
+            pre[a] = summed
+
+        def activate_unit(step, a):
+            summed = pre[a]
+            if a % 2 == 1:
+                nc.scalar.activation(out=summed[:], in_=summed[:], func=ACT.Tanh)
+                return
+            t2 = work.tile([P, PAIR, BATCH], F32, name="t2")
+            gates[a // 2] = t2
+            for e in range(PAIR):
+                c = PAIR * (a // 2) + e
+                nc.scalar.activation(
+                    out=t2[:, e, :], in_=summed[:, e, :], func=ACT.Tanh,
+                    bias=bias_t2[:, c : c + 1], scale=0.5,
+                )
+            if step == STEPS - 1:
+                th = work.tile([P, PAIR, BATCH], F32, name="th")
+                half_tanh[a // 2] = th
+                for e in range(PAIR):
+                    c = PAIR * (a // 2) + e
+                    nc.scalar.activation(
+                        out=th[:, e, :], in_=summed[:, e, :], func=ACT.Tanh,
+                        bias=bias_th[:, c : c + 1], scale=0.5,
+                    )
+
+        def update_chunk(step, G):
+            if step == 0:
+                u = G % 2
+                old = state_bf[:, G // 2, :, PAIR * u : PAIR * (u + 1)].rearrange("p b e -> p e b")
+                new = h1T[:, G]
+            else:
+                old = h1T[:, G]
+                new = work.tile([P, PAIR, BATCH], F32, name="h2T")[:]
+            act = pre[2 * G + 1]
+            diff = work.tile([P, PAIR, BATCH], F32, name="diff")
+            nc.vector.tensor_tensor(out=diff[:], in0=act[:], in1=old, op=ALU.subtract)
+            nc.vector.scalar_tensor_tensor(
+                out=diff[:], in0=gates[G][:], scalar=2.0, in1=diff[:],
+                op0=ALU.subtract, op1=ALU.mult,
+            )
+            for e in range(PAIR):
+                c = PAIR * G + e
+                nc.vector.scalar_tensor_tensor(
+                    out=new[:, e, :], in0=diff[:, e, :], scalar=neg_c[:, c : c + 1],
+                    in1=old[:, e, :], op0=ALU.mult, op1=ALU.add,
+                )
+            if step == STEPS - 1:
+                tauT = half_tanh[G]
+                for e in range(PAIR):
+                    c = PAIR * G + e
+                    nc.vector.tensor_scalar(
+                        out=tauT[:, e, :], in0=tauT[:, e, :],
+                        scalar1=half_tb[:, c : c + 1], scalar2=tb_col[:, c : c + 1],
+                        op0=ALU.mult, op1=ALU.add,
+                    )
+                new_state[G] = (new, tauT[:])
+
+        def round_state(g):
+            nc.vector.tensor_copy(
+                out=state_bf[:, g].rearrange("p b (u e) -> p b u e", u=2),
+                in_=h1T[:, 2 * g : 2 * g + 2].rearrange("p u e b -> p b u e"),
+            )
+
+        def store_chunk(G):
+            natural = work.tile([P, BATCH_TILES, 2, CHUNK], F32, name="natural")
+            results = new_state[G]
+            for t in range(BATCH_TILES):
+                bank = psum_t.tile([P, BANK], F32, name="bank", tag="bank")
+                for which in range(2):
+                    for e in range(PAIR):
+                        slot = 2 * which + e
+                        nc.tensor.transpose(
+                            bank[:, slot * P : (slot + 1) * P],
+                            results[which][:, e, t * P : (t + 1) * P],
+                            ident[:],
+                        )
+                nc.scalar.copy(
+                    out=natural[:, t].rearrange("b w (p e) -> b w p e", e=PAIR),
+                    in_=bank[:].rearrange("b (w e p) -> b w p e", w=2, e=PAIR),
+                )
+            for which, dest in enumerate((out_0, out_1)):
+                nc.sync.dma_start(
+                    out=dest.rearrange("(t b) f -> b t f", b=P)[:, :, G * CHUNK : (G + 1) * CHUNK],
+                    in_=natural[:, :, which, :],
+                )
+
+        def is_unit(a):
+            return 0 <= a < UNITS
+
+        for step in range(STEPS):
+            for tick in range(UNITS + DRAIN):
+                if step == 0 and is_unit(tick):
+                    transpose_unit(tick)
+                    if is_unit(tick + STAGE_BUFS):
+                        load_unit(tick + STAGE_BUFS)
+                if is_unit(tick - 2):
+                    multiply_unit(step, tick - 2)
+                if is_unit(tick - 3):
+                    add_unit(tick - 3)
+                if step == 0 and is_unit(tick - 1):
+                    quantise_unit(tick - 1)
+                if is_unit(tick - 3):
+                    activate_unit(step, tick - 3)
+                if is_unit(tick - 4) and (tick - 4) % 2 == 1:
+                    update_chunk(step, (tick - 4) // 2)
+                if step == 0:
+                    if is_unit(tick - 4) and (tick - 4) % 4 == 3:
+                        round_state((tick - 4) // 4)
+                    if is_unit(tick - 5) and (tick - 5) % 4 == 3:
+                        quantise_state(1, (tick - 5) // 4)
+                elif is_unit(tick - 5) and (tick - 5) % 2 == 1:
+                    store_chunk((tick - 5) // 2)

@@ -42,7 +42,6 @@ def tile_liquidcell_pb_kernel(
         work = ctx.enter_context(tc.tile_pool(name="work", bufs=2))
         psum_t = ctx.enter_context(tc.psum_pool(name="psum_t", bufs=4))
         psum_a = ctx.enter_context(tc.psum_pool(name="psum_a", bufs=4))
-        ctx.enter_context(tc.manual_schedule())
 
         weights = (tau_w_h, W_rec)
         w_codes = [

@@ -42,8 +42,9 @@ def tile_liquidcell_pb_kernel(
         work = ctx.enter_context(tc.tile_pool(name="work", bufs=2))
         psum_t = ctx.enter_context(tc.psum_pool(name="psum_t", bufs=4))
         psum_a = ctx.enter_context(tc.psum_pool(name="psum_a", bufs=4))
+        ctx.enter_context(tc.manual_schedule())
 
-        weights = (tau_w_h, W_rec)
+        weights = (W_rec, tau_w_h)
         w_codes = [
             keep.tile([P, CHUNKS, PASSES, PAIR, P], U32, name="w_codes%d" % w, align_bytes=64)
             for w in range(2)
@@ -64,7 +65,7 @@ def tile_liquidcell_pb_kernel(
         h1T = keep.tile([P, CHUNKS, PAIR, BATCH], F32, name="h1T")
         xT = keep.tile([P, CHUNKS, BATCH * PAIR], BF16, name="xT")
         icT = keep.tile([P, CHUNKS, BATCH * PAIR], BF16, name="icT")
-        addend = (xT, icT)
+        addend = (icT, xT)
 
         ident = keep.tile([P, P], F32, name="ident")
         masks.make_identity(nc, ident[:])
@@ -109,11 +110,26 @@ def tile_liquidcell_pb_kernel(
                 out=h_st[:, :, g * K_PASS : (g + 1) * K_PASS],
                 in_=h_rows[:, :, g * K_PASS : (g + 1) * K_PASS],
             )
-        x_st = load_rows(x_tau.rearrange("(t p) k -> p t k", p=P))
         ic_st = load_rows(input_contrib.rearrange("(t p) k -> p t k", p=P))
+        x_st = load_rows(x_tau.rearrange("(t p) k -> p t k", p=P))
         for a in range(STAGE_BUFS - 3):
             load_unit(a)
 
+        def quantise_state(step, g):
+            nc.vector.quantize_mx(
+                out=s_codes[step][:, g, :].bitcast(FP8X4),
+                scales=s_scales[step][:, g, :],
+                in_=state_bf[:, g].rearrange("p b t -> p (b t)"),
+            )
+
+        state_words = state_bf[:].bitcast(F32)
+        for g in range(PASSES):
+            bank = transpose_bank(h_st[:].bitcast(F32), g)
+            nc.vector.tensor_copy(
+                out=state_words[:, g], in_=bank[:].rearrange("q (u b) -> q b u", u=2)
+            )
+        for g in range(PASSES):
+            quantise_state(0, g)
         vec_bank = psum_t.tile([P, BANK], F32, name="bank", tag="bank")
         nc.tensor.transpose(vec_bank[:, 0:P], vec_rows[:].bitcast(F32), ident[:])
         vecs = keep.tile([P, 4 * CHUNKS], F32, name="vecs")
@@ -140,28 +156,14 @@ def tile_liquidcell_pb_kernel(
             op0=ALU.mult, op1=ALU.add,
         )
 
-        def quantise_state(step, g):
-            nc.vector.quantize_mx(
-                out=s_codes[step][:, g, :].bitcast(FP8X4),
-                scales=s_scales[step][:, g, :],
-                in_=state_bf[:, g].rearrange("p b t -> p (b t)"),
-            )
-
-        state_words = state_bf[:].bitcast(F32)
-        for g in range(PASSES):
-            bank = transpose_bank(h_st[:].bitcast(F32), g)
-            nc.vector.tensor_copy(
-                out=state_words[:, g], in_=bank[:].rearrange("q (u b) -> q b u", u=2)
-            )
-        for staged, dest in ((x_st, xT), (ic_st, icT)):
+        for staged, dest in ((ic_st, icT), (x_st, xT)):
             for i in range(CHUNKS // 2):
                 bank = transpose_bank(staged[:].bitcast(F32), i)
-                nc.scalar.copy(
+                copy = (nc.scalar.copy, nc.vector.tensor_copy)[i % 2]
+                copy(
                     out=dest[:].bitcast(F32)[:, 2 * i : 2 * i + 2, :],
                     in_=bank[:].rearrange("q (v b) -> q v b", v=2),
                 )
-        for g in range(PASSES):
-            quantise_state(0, g)
         for a in range(STAGE_BUFS - 3, STAGE_BUFS):
             load_unit(a)
 
@@ -171,6 +173,7 @@ def tile_liquidcell_pb_kernel(
         gates = {}
         half_tanh = {}
         new_state = {}
+        diffs = {}
 
         def transpose_unit(a):
             words = staged_units[a][:].bitcast(F32)
@@ -218,7 +221,7 @@ def tile_liquidcell_pb_kernel(
 
         def activate_unit(step, a):
             summed = pre[a]
-            if a % 2 == 1:
+            if a % 2 == 0:
                 nc.scalar.activation(out=summed[:], in_=summed[:], func=ACT.Tanh)
                 return
             t2 = work.tile([P, PAIR, BATCH], F32, name="t2")
@@ -239,47 +242,58 @@ def tile_liquidcell_pb_kernel(
                         bias=bias_th[:, c : c + 1], scale=0.5,
                     )
 
-        def update_chunk(step, G):
+        def old_state(step, G):
             if step == 0:
                 u = G % 2
-                old = state_bf[:, G // 2, :, PAIR * u : PAIR * (u + 1)].rearrange("p b e -> p e b")
-                new = h1T[:, G]
-            else:
-                old = h1T[:, G]
-                new = work.tile([P, PAIR, BATCH], F32, name="h2T")[:]
-            act = pre[2 * G + 1]
+                return state_bf[:, G // 2, :, PAIR * u : PAIR * (u + 1)].rearrange("p b e -> p e b")
+            return h1T[:, G]
+
+        def subtract_chunk(step, G):
             diff = work.tile([P, PAIR, BATCH], F32, name="diff")
-            nc.vector.tensor_tensor(out=diff[:], in0=act[:], in1=old, op=ALU.subtract)
+            nc.vector.tensor_tensor(
+                out=diff[:], in0=pre[2 * G][:], in1=old_state(step, G), op=ALU.subtract
+            )
+            diffs[G] = diff
+
+        def gate_chunk(G):
             nc.vector.scalar_tensor_tensor(
-                out=diff[:], in0=gates[G][:], scalar=2.0, in1=diff[:],
+                out=diffs[G][:], in0=gates[G][:], scalar=2.0, in1=diffs[G][:],
                 op0=ALU.subtract, op1=ALU.mult,
             )
+
+        def advance_chunk(step, G):
+            old = old_state(step, G)
+            if step == 0:
+                new = h1T[:, G]
+            else:
+                new = work.tile([P, PAIR, BATCH], F32, name="h2T")[:]
+                new_state[G] = new
             for e in range(PAIR):
                 c = PAIR * G + e
                 nc.vector.scalar_tensor_tensor(
-                    out=new[:, e, :], in0=diff[:, e, :], scalar=neg_c[:, c : c + 1],
+                    out=new[:, e, :], in0=diffs[G][:, e, :], scalar=neg_c[:, c : c + 1],
                     in1=old[:, e, :], op0=ALU.mult, op1=ALU.add,
                 )
-            if step == STEPS - 1:
-                tauT = half_tanh[G]
-                for e in range(PAIR):
-                    c = PAIR * G + e
-                    nc.vector.tensor_scalar(
-                        out=tauT[:, e, :], in0=tauT[:, e, :],
-                        scalar1=half_tb[:, c : c + 1], scalar2=tb_col[:, c : c + 1],
-                        op0=ALU.mult, op1=ALU.add,
-                    )
-                new_state[G] = (new, tauT[:])
+
+        def tau_chunk(G):
+            tauT = half_tanh[G]
+            for e in range(PAIR):
+                c = PAIR * G + e
+                nc.vector.tensor_scalar(
+                    out=tauT[:, e, :], in0=tauT[:, e, :],
+                    scalar1=half_tb[:, c : c + 1], scalar2=tb_col[:, c : c + 1],
+                    op0=ALU.mult, op1=ALU.add,
+                )
 
         def round_state(g):
-            nc.vector.tensor_copy(
-                out=state_bf[:, g].rearrange("p b (u e) -> p b u e", u=2),
-                in_=h1T[:, 2 * g : 2 * g + 2].rearrange("p u e b -> p b u e"),
-            )
+            rounded = state_bf[:, g].rearrange("p b (u e) -> p b u e", u=2)
+            exact = h1T[:, 2 * g : 2 * g + 2].rearrange("p u e b -> p b u e")
+            nc.scalar.copy(out=rounded[:, 0:P], in_=exact[:, 0:P])
+            nc.vector.tensor_copy(out=rounded[:, P:BATCH], in_=exact[:, P:BATCH])
 
         def store_chunk(G):
             natural = work.tile([P, BATCH_TILES, 2, CHUNK], F32, name="natural")
-            results = new_state[G]
+            results = (new_state[G], half_tanh[G][:])
             for t in range(BATCH_TILES):
                 bank = psum_t.tile([P, BANK], F32, name="bank", tag="bank")
                 for which in range(2):
@@ -303,7 +317,13 @@ def tile_liquidcell_pb_kernel(
         def is_unit(a):
             return 0 <= a < UNITS
 
+        def chunk_due(tick, lag):
+            if (tick - lag) % 2 == 0 and 0 <= (tick - lag) // 2 < CHUNKS:
+                return (tick - lag) // 2
+            return None
+
         for step in range(STEPS):
+            last = step == STEPS - 1
             for tick in range(UNITS + DRAIN):
                 if step == 0 and is_unit(tick):
                     transpose_unit(tick)
@@ -311,18 +331,22 @@ def tile_liquidcell_pb_kernel(
                         load_unit(tick + STAGE_BUFS)
                 if is_unit(tick - 2):
                     multiply_unit(step, tick - 2)
+                if last and chunk_due(tick, 7) is not None:
+                    store_chunk(chunk_due(tick, 7))
                 if is_unit(tick - 3):
                     add_unit(tick - 3)
+                if chunk_due(tick, 5) is not None:
+                    subtract_chunk(step, chunk_due(tick, 5))
+                if chunk_due(tick, 6) is not None:
+                    advance_chunk(step, chunk_due(tick, 6))
                 if step == 0 and is_unit(tick - 1):
                     quantise_unit(tick - 1)
+                if last and chunk_due(tick, 6) is not None:
+                    tau_chunk(chunk_due(tick, 6))
                 if is_unit(tick - 3):
                     activate_unit(step, tick - 3)
-                if is_unit(tick - 4) and (tick - 4) % 2 == 1:
-                    update_chunk(step, (tick - 4) // 2)
-                if step == 0:
-                    if is_unit(tick - 4) and (tick - 4) % 4 == 3:
-                        round_state((tick - 4) // 4)
-                    if is_unit(tick - 5) and (tick - 5) % 4 == 3:
-                        quantise_state(1, (tick - 5) // 4)
-                elif is_unit(tick - 5) and (tick - 5) % 2 == 1:
-                    store_chunk((tick - 5) // 2)
+                if chunk_due(tick, 5) is not None:
+                    gate_chunk(chunk_due(tick, 5))
+                if step == 0 and chunk_due(tick, 6) is not None and chunk_due(tick, 6) % 2 == 1:
+                    round_state(chunk_due(tick, 6) // 2)
+                    quantise_state(1, chunk_due(tick, 6) // 2)

@@ -292,7 +292,6 @@ def tile_liquidcell_pb_kernel(
             nc.vector.tensor_copy(out=rounded[:, P:BATCH], in_=exact[:, P:BATCH])
 
         def store_chunk(G):
-            natural = work.tile([P, BATCH_TILES, 2, CHUNK], F32, name="natural")
             results = (new_state[G], half_tanh[G][:])
             for t in range(BATCH_TILES):
                 bank = psum_t.tile([P, BANK], F32, name="bank", tag="bank")
@@ -304,15 +303,16 @@ def tile_liquidcell_pb_kernel(
                             results[which][:, e, t * P : (t + 1) * P],
                             ident[:],
                         )
+                natural = work.tile([P, 2, CHUNK], F32, name="natural", bufs=4)
                 nc.scalar.copy(
-                    out=natural[:, t].rearrange("b w (p e) -> b w p e", e=PAIR),
+                    out=natural[:].rearrange("b w (p e) -> b w p e", e=PAIR),
                     in_=bank[:].rearrange("b (w e p) -> b w p e", w=2, e=PAIR),
                 )
-            for which, dest in enumerate((out_0, out_1)):
-                nc.sync.dma_start(
-                    out=dest.rearrange("(t b) f -> b t f", b=P)[:, :, G * CHUNK : (G + 1) * CHUNK],
-                    in_=natural[:, :, which, :],
-                )
+                for which, dest in enumerate((out_0, out_1)):
+                    nc.sync.dma_start(
+                        out=dest[t * P : (t + 1) * P, G * CHUNK : (G + 1) * CHUNK],
+                        in_=natural[:, which, :],
+                    )
 
         def is_unit(a):
             return 0 <= a < UNITS
@@ -333,20 +333,21 @@ def tile_liquidcell_pb_kernel(
                     multiply_unit(step, tick - 2)
                 if last and chunk_due(tick, 7) is not None:
                     store_chunk(chunk_due(tick, 7))
-                if is_unit(tick - 3):
-                    add_unit(tick - 3)
                 if chunk_due(tick, 5) is not None:
                     subtract_chunk(step, chunk_due(tick, 5))
+                if is_unit(tick - 3):
+                    add_unit(tick - 3)
+                if step == 0 and chunk_due(tick, 7) is not None and chunk_due(tick, 7) % 2 == 1:
+                    quantise_state(1, chunk_due(tick, 7) // 2)
                 if chunk_due(tick, 6) is not None:
                     advance_chunk(step, chunk_due(tick, 6))
                 if step == 0 and is_unit(tick - 1):
                     quantise_unit(tick - 1)
-                if last and chunk_due(tick, 6) is not None:
-                    tau_chunk(chunk_due(tick, 6))
                 if is_unit(tick - 3):
                     activate_unit(step, tick - 3)
+                if last and chunk_due(tick, 6) is not None:
+                    tau_chunk(chunk_due(tick, 6))
                 if chunk_due(tick, 5) is not None:
                     gate_chunk(chunk_due(tick, 5))
                 if step == 0 and chunk_due(tick, 6) is not None and chunk_due(tick, 6) % 2 == 1:
                     round_state(chunk_due(tick, 6) // 2)
-                    quantise_state(1, chunk_due(tick, 6) // 2)

@@ -279,7 +279,7 @@ def tile_liquidcell_pb_kernel(
             tauT = half_tanh[G]
             for e in range(PAIR):
                 c = PAIR * G + e
-                nc.vector.tensor_scalar(
+                nc.gpsimd.tensor_scalar(
                     out=tauT[:, e, :], in0=tauT[:, e, :],
                     scalar1=half_tb[:, c : c + 1], scalar2=tb_col[:, c : c + 1],
                     op0=ALU.mult, op1=ALU.add,

@@ -27,6 +27,7 @@ BANK = 512
 UNITS = 2 * CHUNKS
 STAGE_BUFS = 5
 DRAIN = 6
+EARLY_UNITS = 2
 
 FLOPS = 2 * STEPS * 2 * BATCH * HID * HID
 
@@ -194,29 +195,46 @@ def tile_liquidcell_pb_kernel(
                 in_=grouped[:].rearrange("q g e p t -> q (g e p t)"),
             )
 
+        def multiply_pass(step, a, e, g, out):
+            nc.tensor.matmul_mx(
+                out=out,
+                lhsT=w_codes[a % 2][:, a // 2, g, e, :].bitcast(FP8X4),
+                lhsT_scale=w_scales[a % 2][:, a // 2, g, e, :],
+                rhs=s_codes[step][:, g, :].bitcast(FP8X4),
+                rhs_scale=s_scales[step][:, g, :],
+                start=(g == 0),
+                stop=(g == PASSES - 1),
+            )
+
         def multiply_unit(step, a):
             acc = psum_a.tile([P, PAIR, BATCH], F32, name="acc", tag="acc")
             for e in range(PAIR):
                 for g in range(PASSES):
-                    nc.tensor.matmul_mx(
-                        out=acc[:, e, :],
-                        lhsT=w_codes[a % 2][:, a // 2, g, e, :].bitcast(FP8X4),
-                        lhsT_scale=w_scales[a % 2][:, a // 2, g, e, :],
-                        rhs=s_codes[step][:, g, :].bitcast(FP8X4),
-                        rhs_scale=s_scales[step][:, g, :],
-                        start=(g == 0),
-                        stop=(g == PASSES - 1),
-                    )
-            accs[a] = acc
+                    multiply_pass(step, a, e, g, acc[:, e, :])
+            accs[a] = [acc[:]]
+
+        def multiply_early(step, a):
+            accs[a] = []
+            for e in range(PAIR):
+                bank = psum_t.tile([P, BANK], F32, name="bank", tag="bank")
+                accs[a].append(bank[:, 0:BATCH])
+                for g in range(PASSES - 1):
+                    multiply_pass(step, a, e, g, bank[:, 0:BATCH])
+
+        def multiply_late(step, a):
+            for e in range(PAIR):
+                multiply_pass(step, a, e, PASSES - 1, accs[a][e])
 
         def add_unit(a):
             summed = work.tile([P, PAIR, BATCH], F32, name="summed%d" % (a % 2))
-            nc.vector.tensor_tensor(
-                out=summed[:],
-                in0=accs[a][:],
-                in1=addend[a % 2][:, a // 2, :].rearrange("p (b e) -> p e b", e=PAIR),
-                op=ALU.add,
-            )
+            other = addend[a % 2][:, a // 2, :].rearrange("p (b e) -> p e b", e=PAIR)
+            if len(accs[a]) == 1:
+                nc.vector.tensor_tensor(out=summed[:], in0=accs[a][0], in1=other, op=ALU.add)
+            else:
+                for e in range(PAIR):
+                    nc.vector.tensor_tensor(
+                        out=summed[:, e, :], in0=accs[a][e], in1=other[:, e, :], op=ALU.add
+                    )
             pre[a] = summed
 
         def activate_unit(step, a):
@@ -314,6 +332,27 @@ def tile_liquidcell_pb_kernel(
                         in_=natural[:, which, :],
                     )
 
+        def store_last(which, copy):
+            G = CHUNKS - 1
+            result = (new_state[G], half_tanh[G][:])[which]
+            bank = psum_t.tile([P, BANK], F32, name="bank", tag="bank")
+            for t in range(BATCH_TILES):
+                for e in range(PAIR):
+                    slot = 2 * t + e
+                    nc.tensor.transpose(
+                        bank[:, slot * P : (slot + 1) * P], result[:, e, t * P : (t + 1) * P], ident[:]
+                    )
+            natural = work.tile([P, 2, CHUNK], F32, name="natural", bufs=4)
+            copy(
+                out=natural[:].rearrange("b t (p e) -> b t p e", e=PAIR),
+                in_=bank[:].rearrange("b (t e p) -> b t p e", t=2, e=PAIR),
+            )
+            dest = (out_0, out_1)[which]
+            for t in range(BATCH_TILES):
+                nc.sync.dma_start(
+                    out=dest[t * P : (t + 1) * P, G * CHUNK : (G + 1) * CHUNK], in_=natural[:, t, :]
+                )
+
         def is_unit(a):
             return 0 <= a < UNITS
 
@@ -330,9 +369,19 @@ def tile_liquidcell_pb_kernel(
                     if is_unit(tick + STAGE_BUFS):
                         load_unit(tick + STAGE_BUFS)
                 if is_unit(tick - 2):
-                    multiply_unit(step, tick - 2)
+                    if last and tick - 2 < EARLY_UNITS:
+                        multiply_late(step, tick - 2)
+                    else:
+                        multiply_unit(step, tick - 2)
+                if step == 0 and tick == UNITS + 2:
+                    for a in range(EARLY_UNITS):
+                        multiply_early(step + 1, a)
                 if last and chunk_due(tick, 7) is not None:
-                    store_chunk(chunk_due(tick, 7))
+                    if chunk_due(tick, 7) < CHUNKS - 1:
+                        store_chunk(chunk_due(tick, 7))
+                    else:
+                        store_last(1, nc.scalar.copy)
+                        store_last(0, nc.vector.tensor_copy)
                 if chunk_due(tick, 5) is not None:
                     subtract_chunk(step, chunk_due(tick, 5))
                 if is_unit(tick - 3):

@@ -28,6 +28,7 @@ UNITS = 2 * CHUNKS
 STAGE_BUFS = 5
 DRAIN = 6
 EARLY_UNITS = 2
+SHARED_UNITS = 5
 
 FLOPS = 2 * STEPS * 2 * BATCH * HID * HID
 
@@ -176,16 +177,27 @@ def tile_liquidcell_pb_kernel(
         new_state = {}
         diffs = {}
 
+        shared_banks = {}
+
         def transpose_unit(a):
             words = staged_units[a][:].bitcast(F32)
             grouped = group.tile([P, PASSES, PAIR, P, 2 * PAIR], BF16, name="grouped", align_bytes=64)
+            grouped_units[a] = grouped
             for g in range(PASSES):
                 bank = transpose_bank(words, g)
-                nc.scalar.copy(
-                    out=grouped[:].bitcast(F32)[:, g],
-                    in_=bank[:].rearrange("q (u e p) -> q e p u", u=2, e=PAIR),
-                )
-            grouped_units[a] = grouped
+                if g == 0 and a < SHARED_UNITS:
+                    shared_banks[a] = bank
+                else:
+                    nc.scalar.copy(
+                        out=grouped[:].bitcast(F32)[:, g],
+                        in_=bank[:].rearrange("q (u e p) -> q e p u", u=2, e=PAIR),
+                    )
+
+        def empty_shared_bank(a):
+            nc.vector.tensor_copy(
+                out=grouped_units[a][:].bitcast(F32)[:, 0],
+                in_=shared_banks[a][:].rearrange("q (u e p) -> q e p u", u=2, e=PAIR),
+            )
 
         def quantise_unit(a):
             grouped = grouped_units[a]
@@ -373,7 +385,7 @@ def tile_liquidcell_pb_kernel(
                         multiply_late(step, tick - 2)
                     else:
                         multiply_unit(step, tick - 2)
-                if step == 0 and tick == UNITS + 2:
+                if step == 0 and tick == UNITS + 4:
                     for a in range(EARLY_UNITS):
                         multiply_early(step + 1, a)
                 if last and chunk_due(tick, 7) is not None:
@@ -386,8 +398,12 @@ def tile_liquidcell_pb_kernel(
                     subtract_chunk(step, chunk_due(tick, 5))
                 if is_unit(tick - 3):
                     add_unit(tick - 3)
-                if step == 0 and chunk_due(tick, 7) is not None and chunk_due(tick, 7) % 2 == 1:
-                    quantise_state(1, chunk_due(tick, 7) // 2)
+                if step == 0 and tick < SHARED_UNITS:
+                    empty_shared_bank(tick)
+                if step == 0 and chunk_due(tick, 9) in (1, 3, 5):
+                    quantise_state(1, chunk_due(tick, 9) // 2)
+                if step == 0 and chunk_due(tick, 7) == CHUNKS - 1:
+                    quantise_state(1, PASSES - 1)
                 if chunk_due(tick, 6) is not None:
                     advance_chunk(step, chunk_due(tick, 6))
                 if step == 0 and is_unit(tick - 1):

@@ -319,7 +319,8 @@ def tile_liquidcell_pb_kernel(
             rounded = state_bf[:, g].rearrange("p b (u e) -> p b u e", u=2)
             exact = h1T[:, 2 * g : 2 * g + 2].rearrange("p u e b -> p b u e")
             nc.scalar.copy(out=rounded[:, 0:P], in_=exact[:, 0:P])
-            nc.vector.tensor_copy(out=rounded[:, P:BATCH], in_=exact[:, P:BATCH])
+            second = nc.scalar.copy if g == PASSES - 2 else nc.vector.tensor_copy
+            second(out=rounded[:, P:BATCH], in_=exact[:, P:BATCH])
 
         def store_chunk(G):
             results = (new_state[G], half_tanh[G][:])

from contextlib import ExitStack
import math

import concourse.masks as masks
import concourse.mybir as mybir

F32 = mybir.dt.float32
BF16 = mybir.dt.bfloat16
U32 = mybir.dt.uint32
U8 = mybir.dt.uint8
FP8X4 = mybir.dt.float8_e4m3fn_x4
ALU = mybir.AluOpType
ACT = mybir.ActivationFunctionType

P = 128
BATCH = 256
HID = 2048
DT = 0.1
STEPS = 2
BATCH_TILES = BATCH // P
PAIR = 2
K_PASS = 4 * P
PASSES = HID // K_PASS
CHUNK = PAIR * P
CHUNKS = HID // CHUNK
BANK = 512
UNITS = 2 * CHUNKS
STAGE_BUFS = 5
DRAIN = 6
EARLY_UNITS = 2
SHARED_UNITS = 5

FLOPS = 2 * STEPS * 2 * BATCH * HID * HID


def tile_liquidcell_pb_kernel(
    tc, h, input_contrib, x_tau, W_rec, tau_w_h, tau_adapt_b, tau_base, out_0, out_1
):
    nc = tc.nc
    with ExitStack() as ctx:
        keep = ctx.enter_context(tc.tile_pool(name="keep", bufs=1))
        stage = ctx.enter_context(tc.tile_pool(name="stage", bufs=STAGE_BUFS))
        group = ctx.enter_context(tc.tile_pool(name="group", bufs=2))
        work = ctx.enter_context(tc.tile_pool(name="work", bufs=2))
        psum_t = ctx.enter_context(tc.psum_pool(name="psum_t", bufs=4))
        psum_a = ctx.enter_context(tc.psum_pool(name="psum_a", bufs=4))
        ctx.enter_context(tc.manual_schedule())

        weights = (W_rec, tau_w_h)
        w_codes = [
            keep.tile([P, CHUNKS, PASSES, PAIR, P], U32, name="w_codes%d" % w, align_bytes=64)
            for w in range(2)
        ]
        w_scales = [
            keep.tile([P, CHUNKS, PASSES, PAIR, P], U8, name="w_scales%d" % w, align_bytes=64)
            for w in range(2)
        ]
        s_codes = [
            keep.tile([P, PASSES, BATCH], U32, name="s_codes%d" % s, align_bytes=64)
            for s in range(STEPS)
        ]
        s_scales = [
            keep.tile([P, PASSES, BATCH], U8, name="s_scales%d" % s, align_bytes=64)
            for s in range(STEPS)
        ]
        state_bf = keep.tile([P, PASSES, BATCH, 2 * PAIR], BF16, name="state_bf", align_bytes=64)
        h1T = keep.tile([P, CHUNKS, PAIR, BATCH], F32, name="h1T")
        xT = keep.tile([P, CHUNKS, BATCH * PAIR], BF16, name="xT")
        icT = keep.tile([P, CHUNKS, BATCH * PAIR], BF16, name="icT")
        addend = (icT, xT)

        ident = keep.tile([P, P], F32, name="ident")
        masks.make_identity(nc, ident[:])

        def transpose_bank(words, i):
            bank = psum_t.tile([P, BANK], F32, name="bank", tag="bank")
            for v in range(2):
                for r in range(2):
                    slot = 2 * v + r
                    block = 2 * i + v
                    nc.tensor.transpose(
                        bank[:, slot * P : (slot + 1) * P],
                        words[:, r, block * P : (block + 1) * P],
                        ident[:],
                    )
            return bank

        vec_rows = keep.tile([P, PAIR * P], BF16, name="vec_rows")
        nc.vector.memset(vec_rows[:], 0.0)
        nc.scalar.dma_start(
            out=vec_rows[0:CHUNKS, :], in_=tau_adapt_b.rearrange("(g w) -> g w", g=CHUNKS)
        )
        nc.scalar.dma_start(
            out=vec_rows[CHUNKS : 2 * CHUNKS, :], in_=tau_base.rearrange("(g w) -> g w", g=CHUNKS)
        )

        def load_rows(rows):
            staged = stage.tile([P, 2, HID], BF16, name="staged", tag="staged")
            nc.sync.dma_start(out=staged[:], in_=rows)
            return staged

        staged_units = {}

        def load_unit(a):
            rows = weights[a % 2][(a // 2) * CHUNK : (a // 2 + 1) * CHUNK, :]
            staged_units[a] = load_rows(rows.rearrange("(p e) k -> p e k", e=PAIR))

        h_st = stage.tile([P, 2, HID], BF16, name="staged", tag="staged")
        h_rows = h.rearrange("(t p) k -> p t k", p=P)
        for g in range(PASSES):
            nc.sync.dma_start(
                out=h_st[:, :, g * K_PASS : (g + 1) * K_PASS],
                in_=h_rows[:, :, g * K_PASS : (g + 1) * K_PASS],
            )
        ic_st = load_rows(input_contrib.rearrange("(t p) k -> p t k", p=P))
        x_st = load_rows(x_tau.rearrange("(t p) k -> p t k", p=P))
        for a in range(STAGE_BUFS - 3):
            load_unit(a)

        def quantise_state(step, g):
            nc.vector.quantize_mx(
                out=s_codes[step][:, g, :].bitcast(FP8X4),
                scales=s_scales[step][:, g, :],
                in_=state_bf[:, g].rearrange("p b t -> p (b t)"),
            )

        state_words = state_bf[:].bitcast(F32)
        for g in range(PASSES):
            bank = transpose_bank(h_st[:].bitcast(F32), g)
            nc.vector.tensor_copy(
                out=state_words[:, g], in_=bank[:].rearrange("q (u b) -> q b u", u=2)
            )
        for g in range(PASSES):
            quantise_state(0, g)
        vec_bank = psum_t.tile([P, BANK], F32, name="bank", tag="bank")
        nc.tensor.transpose(vec_bank[:, 0:P], vec_rows[:].bitcast(F32), ident[:])
        vecs = keep.tile([P, 4 * CHUNKS], F32, name="vecs")
        nc.vector.tensor_copy(out=vecs[:], in_=vec_bank[:, 0 : 2 * CHUNKS].bitcast(BF16))
        b_col = vecs[:, 0 : 2 * CHUNKS]
        tb_col = vecs[:, 2 * CHUNKS : 4 * CHUNKS]
        bias_th = keep.tile([P, 2 * CHUNKS], F32, name="bias_th")
        bias_t2 = keep.tile([P, 2 * CHUNKS], F32, name="bias_t2")
        half_tb = keep.tile([P, 2 * CHUNKS], F32, name="half_tb")
        neg_c = keep.tile([P, 2 * CHUNKS], F32, name="neg_c")
        nc.vector.tensor_scalar(
            out=bias_th[:], in0=b_col, scalar1=0.5, scalar2=0.0, op0=ALU.mult, op1=ALU.add
        )
        nc.vector.tensor_scalar(
            out=bias_t2[:], in0=b_col, scalar1=0.5, scalar2=0.5 * math.log(3.0),
            op0=ALU.mult, op1=ALU.add,
        )
        nc.vector.tensor_scalar(
            out=half_tb[:], in0=tb_col, scalar1=0.5, scalar2=0.0, op0=ALU.mult, op1=ALU.add
        )
        nc.vector.reciprocal(out=neg_c[:], in_=tb_col)
        nc.vector.tensor_scalar(
            out=neg_c[:], in0=neg_c[:], scalar1=-DT * 2.0 / 3.0, scalar2=0.0,
            op0=ALU.mult, op1=ALU.add,
        )

        for staged, dest in ((ic_st, icT), (x_st, xT)):
            for i in range(CHUNKS // 2):
                bank = transpose_bank(staged[:].bitcast(F32), i)
                copy = (nc.scalar.copy, nc.vector.tensor_copy)[i % 2]
                copy(
                    out=dest[:].bitcast(F32)[:, 2 * i : 2 * i + 2, :],
                    in_=bank[:].rearrange("q (v b) -> q v b", v=2),
                )
        for a in range(STAGE_BUFS - 3, STAGE_BUFS):
            load_unit(a)

        grouped_units = {}
        accs = {}
        pre = {}
        gates = {}
        half_tanh = {}
        new_state = {}
        diffs = {}

        shared_banks = {}

        def transpose_unit(a):
            words = staged_units[a][:].bitcast(F32)
            grouped = group.tile([P, PASSES, PAIR, P, 2 * PAIR], BF16, name="grouped", align_bytes=64)
            grouped_units[a] = grouped
            for g in range(PASSES):
                bank = transpose_bank(words, g)
                if g == 0 and a < SHARED_UNITS:
                    shared_banks[a] = bank
                else:
                    nc.scalar.copy(
                        out=grouped[:].bitcast(F32)[:, g],
                        in_=bank[:].rearrange("q (u e p) -> q e p u", u=2, e=PAIR),
                    )

        def empty_shared_bank(a):
            nc.vector.tensor_copy(
                out=grouped_units[a][:].bitcast(F32)[:, 0],
                in_=shared_banks[a][:].rearrange("q (u e p) -> q e p u", u=2, e=PAIR),
            )

        def quantise_unit(a):
            grouped = grouped_units[a]
            nc.vector.quantize_mx(
                out=w_codes[a % 2][:, a // 2].rearrange("q g e p -> q (g e p)").bitcast(FP8X4),
                scales=w_scales[a % 2][:, a // 2].rearrange("q g e p -> q (g e p)"),
                in_=grouped[:].rearrange("q g e p t -> q (g e p t)"),
            )

        def multiply_pass(step, a, e, g, out):
            nc.tensor.matmul_mx(
                out=out,
                lhsT=w_codes[a % 2][:, a // 2, g, e, :].bitcast(FP8X4),
                lhsT_scale=w_scales[a % 2][:, a // 2, g, e, :],
                rhs=s_codes[step][:, g, :].bitcast(FP8X4),
                rhs_scale=s_scales[step][:, g, :],
                start=(g == 0),
                stop=(g == PASSES - 1),
            )

        def multiply_unit(step, a):
            acc = psum_a.tile([P, PAIR, BATCH], F32, name="acc", tag="acc")
            for e in range(PAIR):
                for g in range(PASSES):
                    multiply_pass(step, a, e, g, acc[:, e, :])
            accs[a] = [acc[:]]

        def multiply_early(step, a):
            accs[a] = []
            for e in range(PAIR):
                bank = psum_t.tile([P, BANK], F32, name="bank", tag="bank")
                accs[a].append(bank[:, 0:BATCH])
                for g in range(PASSES - 1):
                    multiply_pass(step, a, e, g, bank[:, 0:BATCH])

        def multiply_late(step, a):
            for e in range(PAIR):
                multiply_pass(step, a, e, PASSES - 1, accs[a][e])

        def add_unit(a):
            summed = work.tile([P, PAIR, BATCH], F32, name="summed%d" % (a % 2))
            other = addend[a % 2][:, a // 2, :].rearrange("p (b e) -> p e b", e=PAIR)
            if len(accs[a]) == 1:
                nc.vector.tensor_tensor(out=summed[:], in0=accs[a][0], in1=other, op=ALU.add)
            else:
                for e in range(PAIR):
                    nc.vector.tensor_tensor(
                        out=summed[:, e, :], in0=accs[a][e], in1=other[:, e, :], op=ALU.add
                    )
            pre[a] = summed

        def activate_unit(step, a):
            summed = pre[a]
            if a % 2 == 0:
                nc.scalar.activation(out=summed[:], in_=summed[:], func=ACT.Tanh)
                return
            t2 = work.tile([P, PAIR, BATCH], F32, name="t2")
            gates[a // 2] = t2
            for e in range(PAIR):
                c = PAIR * (a // 2) + e
                nc.scalar.activation(
                    out=t2[:, e, :], in_=summed[:, e, :], func=ACT.Tanh,
                    bias=bias_t2[:, c : c + 1], scale=0.5,
                )
            if step == STEPS - 1:
                th = work.tile([P, PAIR, BATCH], F32, name="th")
                half_tanh[a // 2] = th
                for e in range(PAIR):
                    c = PAIR * (a // 2) + e
                    nc.scalar.activation(
                        out=th[:, e, :], in_=summed[:, e, :], func=ACT.Tanh,
                        bias=bias_th[:, c : c + 1], scale=0.5,
                    )

        def old_state(step, G):
            if step == 0:
                u = G % 2
                return state_bf[:, G // 2, :, PAIR * u : PAIR * (u + 1)].rearrange("p b e -> p e b")
            return h1T[:, G]

        def subtract_chunk(step, G):
            diff = work.tile([P, PAIR, BATCH], F32, name="diff")
            nc.vector.tensor_tensor(
                out=diff[:], in0=pre[2 * G][:], in1=old_state(step, G), op=ALU.subtract
            )
            diffs[G] = diff

        def gate_chunk(G):
            nc.vector.scalar_tensor_tensor(
                out=diffs[G][:], in0=gates[G][:], scalar=2.0, in1=diffs[G][:],
                op0=ALU.subtract, op1=ALU.mult,
            )

        def advance_chunk(step, G):
            old = old_state(step, G)
            if step == 0:
                new = h1T[:, G]
            else:
                new = work.tile([P, PAIR, BATCH], F32, name="h2T")[:]
                new_state[G] = new
            for e in range(PAIR):
                c = PAIR * G + e
                nc.vector.scalar_tensor_tensor(
                    out=new[:, e, :], in0=diffs[G][:, e, :], scalar=neg_c[:, c : c + 1],
                    in1=old[:, e, :], op0=ALU.mult, op1=ALU.add,
                )

        def tau_chunk(G):
            tauT = half_tanh[G]
            for e in range(PAIR):
                c = PAIR * G + e
                nc.gpsimd.tensor_scalar(
                    out=tauT[:, e, :], in0=tauT[:, e, :],
                    scalar1=half_tb[:, c : c + 1], scalar2=tb_col[:, c : c + 1],
                    op0=ALU.mult, op1=ALU.add,
                )

        def round_state(g):
            rounded = state_bf[:, g].rearrange("p b (u e) -> p b u e", u=2)
            exact = h1T[:, 2 * g : 2 * g + 2].rearrange("p u e b -> p b u e")
            nc.scalar.copy(out=rounded[:, 0:P], in_=exact[:, 0:P])
            second = nc.scalar.copy if g == PASSES - 2 else nc.vector.tensor_copy
            second(out=rounded[:, P:BATCH], in_=exact[:, P:BATCH])

        def store_chunk(G):
            results = (new_state[G], half_tanh[G][:])
            for t in range(BATCH_TILES):
                bank = psum_t.tile([P, BANK], F32, name="bank", tag="bank")
                for which in range(2):
                    for e in range(PAIR):
                        slot = 2 * which + e
                        nc.tensor.transpose(
                            bank[:, slot * P : (slot + 1) * P],
                            results[which][:, e, t * P : (t + 1) * P],
                            ident[:],
                        )
                natural = work.tile([P, 2, CHUNK], F32, name="natural", bufs=4)
                nc.scalar.copy(
                    out=natural[:].rearrange("b w (p e) -> b w p e", e=PAIR),
                    in_=bank[:].rearrange("b (w e p) -> b w p e", w=2, e=PAIR),
                )
                for which, dest in enumerate((out_0, out_1)):
                    nc.sync.dma_start(
                        out=dest[t * P : (t + 1) * P, G * CHUNK : (G + 1) * CHUNK],
                        in_=natural[:, which, :],
                    )

        def store_last(which, copy):
            G = CHUNKS - 1
            result = (new_state[G], half_tanh[G][:])[which]
            bank = psum_t.tile([P, BANK], F32, name="bank", tag="bank")
            for t in range(BATCH_TILES):
                for e in range(PAIR):
                    slot = 2 * t + e
                    nc.tensor.transpose(
                        bank[:, slot * P : (slot + 1) * P], result[:, e, t * P : (t + 1) * P], ident[:]
                    )
            natural = work.tile([P, 2, CHUNK], F32, name="natural", bufs=4)
            copy(
                out=natural[:].rearrange("b t (p e) -> b t p e", e=PAIR),
                in_=bank[:].rearrange("b (t e p) -> b t p e", t=2, e=PAIR),
            )
            dest = (out_0, out_1)[which]
            for t in range(BATCH_TILES):
                nc.sync.dma_start(
                    out=dest[t * P : (t + 1) * P, G * CHUNK : (G + 1) * CHUNK], in_=natural[:, t, :]
                )

        def is_unit(a):
            return 0 <= a < UNITS

        def chunk_due(tick, lag):
            if (tick - lag) % 2 == 0 and 0 <= (tick - lag) // 2 < CHUNKS:
                return (tick - lag) // 2
            return None

        for step in range(STEPS):
            last = step == STEPS - 1
            for tick in range(UNITS + DRAIN):
                if step == 0 and is_unit(tick):
                    transpose_unit(tick)
                    if is_unit(tick + STAGE_BUFS):
                        load_unit(tick + STAGE_BUFS)
                if is_unit(tick - 2):
                    if last and tick - 2 < EARLY_UNITS:
                        multiply_late(step, tick - 2)
                    else:
                        multiply_unit(step, tick - 2)
                if step == 0 and tick == UNITS + 4:
                    for a in range(EARLY_UNITS):
                        multiply_early(step + 1, a)
                if last and chunk_due(tick, 7) is not None:
                    if chunk_due(tick, 7) < CHUNKS - 1:
                        store_chunk(chunk_due(tick, 7))
                    else:
                        store_last(1, nc.scalar.copy)
                        store_last(0, nc.vector.tensor_copy)
                if chunk_due(tick, 5) is not None:
                    subtract_chunk(step, chunk_due(tick, 5))
                if is_unit(tick - 3):
                    add_unit(tick - 3)
                if step == 0 and tick < SHARED_UNITS:
                    empty_shared_bank(tick)
                if step == 0 and chunk_due(tick, 9) in (1, 3, 5):
                    quantise_state(1, chunk_due(tick, 9) // 2)
                if step == 0 and chunk_due(tick, 7) == CHUNKS - 1:
                    quantise_state(1, PASSES - 1)
                if chunk_due(tick, 6) is not None:
                    advance_chunk(step, chunk_due(tick, 6))
                if step == 0 and is_unit(tick - 1):
                    quantise_unit(tick - 1)
                if is_unit(tick - 3):
                    activate_unit(step, tick - 3)
                if last and chunk_due(tick, 6) is not None:
                    tau_chunk(chunk_due(tick, 6))
                if chunk_due(tick, 5) is not None:
                    gate_chunk(chunk_due(tick, 5))
                if step == 0 and chunk_due(tick, 6) is not None and chunk_due(tick, 6) % 2 == 1:
                    round_state(chunk_due(tick, 6) // 2)
